import numpy as np
import ml_dtypes


def mxq(x, axis, fmt="e4m3"):
    dtype, down = {"e4m3": (ml_dtypes.float8_e4m3fn, 7), "e5m2": (ml_dtypes.float8_e5m2, 14)}[fmt]
    v = np.moveaxis(np.asarray(x, np.float32).astype(ml_dtypes.bfloat16).astype(np.float64), axis, -1)
    blocks = v.reshape(v.shape[:-1] + (-1, 32))
    amax = np.abs(blocks).max(-1, keepdims=True)
    byte = np.maximum(np.where(amax > 0, np.frexp(amax)[1] - 1 + 127, 0) - down, 1)
    scale = np.exp2(byte - 127.0)
    codes = (blocks / scale).astype(np.float32).astype(dtype).astype(np.float64)
    return np.moveaxis((codes * scale).reshape(v.shape), -1, axis)


WIDE = False


def mx_kscale(k):
    if not WIDE:
        return np.ones(k)
    levels = np.array([30, -30])
    if k % 512:
        return np.exp2(np.random.permutation(np.resize(levels, k // 32))).repeat(32)
    a = np.empty((k // 512, 16))
    for p in range(k // 512):
        a[p, :8] = np.random.permutation(np.resize(levels, 8))
        for g in range(8):
            far = levels[np.abs(levels - a[p, g]) >= 10]
            a[p, g + 8] = far[np.random.randint(len(far))]
    return np.exp2(a.ravel()).repeat(32)


BF16 = ml_dtypes.bfloat16


def bf(x):
    return np.asarray(x, np.float32).astype(BF16)


def f64(x):
    return np.asarray(x).astype(np.float64)


B, S, H, D = 2, 512, 4, 512

EPS = 2.0 ** -23


def rms_normalize(v):
    ms = np.mean(v * v, axis=-1, keepdims=True)
    return v / np.sqrt(ms + EPS)


def sigmoid(v):
    return 1.0 / (1.0 + np.exp(-v))


def setup_inputs():
    s = mx_kscale(D)
    return {"embeddings": bf(np.random.standard_normal((B, S, D)) * s),
            "hidden_states": bf(np.random.standard_normal((B, S, H, D))),
            "Wv": bf(np.random.standard_normal((D, D)) / np.sqrt(D) / s),
            "bv": bf(np.random.standard_normal(D) * 0.5),
            "Wk": bf(np.random.standard_normal((H, D, D)) / np.sqrt(D) / s),
            "bk": bf(np.random.standard_normal((H, D)) * 0.5),
            "g1": bf(1.0 + 0.3 * np.random.standard_normal((H, D))),
            "g2": bf(1.0 + 0.3 * np.random.standard_normal((H, D)))}


def reference(embeddings, hidden_states, Wv, bv, Wk, bk, g1, g2):
    eq = mxq(f64(embeddings), 2, "e5m2")
    wkq = mxq(f64(Wk), 2, "e4m3")
    key = (eq @ wkq.reshape(H * D, D).T).reshape(B, S, H, D) + f64(bk)
    normed_key = rms_normalize(key) * f64(g1)
    normed_query = rms_normalize(f64(hidden_states)) * f64(g2)
    gate = np.sum(normed_key * normed_query, axis=-1) / np.sqrt(D)
    gate = np.sqrt(np.maximum(np.abs(gate), 1e-6)) * np.sign(gate)
    gate = sigmoid(gate)[..., None]
    value = ((eq @ mxq(f64(Wv), 1, "e4m3").T) + f64(bv))[:, :, None, :]
    return gate * value

@@ -1,0 +1,363 @@
+from contextlib import ExitStack
+import math
+
+import concourse.mybir as mybir
+from concourse.masks import make_identity
+
+FLOPS = 2 * 1024 * 512 * 2560
+
+F32 = mybir.dt.float32
+BF16 = mybir.dt.bfloat16
+U32 = mybir.dt.uint32
+U8 = mybir.dt.uint8
+E5M2 = mybir.dt.float8_e5m2_x4
+E4M3 = mybir.dt.float8_e4m3fn_x4
+ACT = mybir.ActivationFunctionType
+ALU = mybir.AluOpType
+AX = mybir.AxisListType
+
+P = 128
+D = 512
+H = 4
+EPS = 2.0 ** -23
+C1 = 1.0 / math.sqrt(512.0)
+C2 = EPS * math.sqrt(512.0)
+CMIN = math.sqrt(1e-6)
+
+
+KW_V_FROM = 4
+
+
+def tile_engramgating_kernel(tc, embeddings, hidden_states, Wv, bv, Wk, bk, g1, g2, out):
+    nc = tc.nc
+    with ExitStack() as ctx:
+        keep = ctx.enter_context(tc.tile_pool(name="keep", bufs=1))
+        work = ctx.enter_context(tc.tile_pool(name="work", bufs=2))
+        psum = ctx.enter_context(tc.psum_pool(name="psum", bufs=1))
+        ctx.enter_context(tc.manual_schedule())
+
+        ev = embeddings.rearrange("b s k -> (b s) k").rearrange("(g p t) k -> g p t k", g=2, p=P, t=4)
+        hv = hidden_states.rearrange("b s h d -> (b s) (h d)").rearrange("(g p t) c -> g t p c", g=2, p=P, t=4)
+        ov = out.rearrange("b s h d -> (b s) h d").rearrange("(g p t) h d -> g p t h d", g=2, p=P, t=4)
+
+        craw = keep.tile([P, P], BF16, name="craw")
+        nc.gpsimd.memset(craw[:], 0.0)
+        for v, vec in enumerate((bk, g1, g2)):
+            nc.scalar.dma_start(out=craw[16 * v:16 * (v + 1), :], in_=vec.rearrange("h (c p) -> (h c) p", p=P))
+        warm = keep.tile([P, 1], F32, name="warm")
+        nc.gpsimd.memset(warm[:], 0.0)
+        warm2 = keep.tile([P, 1], F32, name="warm2")
+        nc.scalar.activation(out=warm2[:], in_=warm[:], func=ACT.Sigmoid)
+        ident_f = keep.tile([P, P], F32, name="ident_f")
+        make_identity(nc, ident_f[:])
+        ident_b = keep.tile([P, P], BF16, name="ident_b")
+        make_identity(nc, ident_b[:])
+        quarter = keep.tile([P, 4], F32, name="quarter")
+        nc.gpsimd.memset(quarter[:], 0.25)
+        mone = keep.tile([P, 8], F32, name="mone")
+        nc.gpsimd.memset(mone[:], -1.0)
+        bvb = keep.tile([P, D], BF16, name="bvb")
+
+        e_codes = [keep.tile([P, D], U32, name="e_codes%d" % g, align_bytes=64) for g in range(2)]
+        e_scales = [keep.tile([P, D], U8, name="e_scales%d" % g, align_bytes=64) for g in range(2)]
+        w_codes = [keep.tile([P, D], U32, name="w_codes%d" % i, align_bytes=64) for i in range(5)]
+        w_scales = [keep.tile([P, D], U8, name="w_scales%d" % i, align_bytes=64) for i in range(5)]
+
+        hs = [[None] * 4, [None] * 4]
+        raws = {}
+
+        def load_hs(g, t):
+            tl = keep.tile([P, H * D], BF16, name="hs%d_%d" % (g, t))
+            nc.sync.dma_start(out=tl[:], in_=hv[g, t])
+            hs[g][t] = tl
+
+        def load_rows(kind, i):
+            if kind == "e":
+                view = ev[i]
+            else:
+                view = (Wv if i == 4 else Wk[i]).rearrange("(c p) k -> p c k", p=P)
+            for a in range(2):
+                tl = work.tile([P, 2, D], BF16, name="raw%s%d_%d" % (kind, i, a), tag="raw", bufs=14)
+                nc.sync.dma_start(out=tl[:], in_=view[:, 2 * a:2 * a + 2, :])
+                raws[(kind, i, a)] = tl
+
+        load_hs(0, 0)
+        load_rows("e", 0)
+        load_rows("w", 0)
+        load_rows("w", 1)
+        load_hs(0, 1)
+        load_rows("w", 2)
+        load_hs(0, 2)
+        load_hs(0, 3)
+        load_rows("w", 4)
+        nc.sync.dma_start(out=bvb[:], in_=bv.partition_broadcast(P))
+        load_rows("w", 3)
+        load_rows("e", 1)
+        for t in range(4):
+            load_hs(1, t)
+
+        def prep(kind, i, copy_on_scalar):
+            codes, scales, fmt = (e_codes[i], e_scales[i], E5M2) if kind == "e" else (w_codes[i], w_scales[i], E4M3)
+            xts = []
+            for a in range(2):
+                words = raws[(kind, i, a)][:].rearrange("p t k -> p (t k)").bitcast(F32)
+                xt = psum.tile([P, D], F32, name="xt%s%d_%d" % (kind, i, a), tag="kb", bufs=3)
+                for tt in range(2):
+                    for u in range(2):
+                        j = 2 * tt + u
+                        nc.tensor.transpose(xt[:, j * P:(j + 1) * P], words[:, 256 * tt + u:256 * (tt + 1):2], ident_f[:])
+                xts.append(xt)
+            grps = []
+            for a in range(2):
+                grp = work.tile([P, 1024], BF16, name="grp%s%d_%d" % (kind, i, a), tag="grp", bufs=4, align_bytes=64)
+                dst = grp[:].bitcast(F32).rearrange("p (tt r u) -> p tt r u", tt=2, u=2)
+                srcv = xts[a][:].rearrange("p (tt u r) -> p tt r u", tt=2, u=2)
+                if copy_on_scalar:
+                    nc.scalar.copy(out=dst, in_=srcv)
+                else:
+                    nc.vector.tensor_copy(out=dst, in_=srcv)
+                grps.append(grp)
+            for a in range(2):
+                cols = slice(256 * a, 256 * (a + 1))
+                nc.vector.quantize_mx(out=codes[:, cols].bitcast(fmt), scales=scales[:, cols], in_=grps[a][:])
+
+        st8s = [keep.tile([P, 8], F32, name="st8_%d" % n) for n in range(8)]
+        vals = [keep.tile([P, 4, D], F32, name="val%d" % g) for g in range(2)]
+        pts, sqs, kws, tiny = {}, {}, {}, {}
+
+        def small(nm, n, w):
+            tl = keep.tile([P, w], F32, name="%s_%d" % (nm, n))
+            tiny[(nm, n)] = tl
+            return tl
+
+        def consts():
+            cps = psum.tile([P, P], BF16, name="cps", tag="kb", bufs=3)
+            nc.tensor.transpose(cps[:], craw[:], ident_b[:])
+            cst = keep.tile([P, 48], F32, name="cst")
+            nc.vector.tensor_copy(out=cst[:], in_=cps[:, 0:48])
+            w16 = keep.tile([P, 16], F32, name="w16")
+            nc.vector.tensor_tensor(out=w16[:], in0=cst[:, 16:32], in1=cst[:, 32:48], op=ALU.mult)
+            wbk = keep.tile([P, 16], F32, name="wbk")
+            nc.vector.tensor_tensor(out=wbk[:], in0=w16[:], in1=cst[:, 0:16], op=ALU.mult)
+            return cst, w16, wbk
+
+        def ssq(n, t):
+            g, h = divmod(n, 4)
+            junk = work.tile([P, D], F32, name="js%d_%d" % (n, t), tag="junks", bufs=2)
+            nc.scalar.activation(
+                out=junk[:], in_=hs[g][t][:, h * D:(h + 1) * D], func=ACT.Square, accum_out=st8s[n][:, 4 + t:5 + t]
+            )
+
+        def mx(n):
+            g, h = divmod(n, 4)
+            for c in range(4):
+                pt = psum.tile([P, D], F32, name="pt%d_%d" % (n, c), tag="pt", bufs=4)
+                nc.tensor.matmul_mx(
+                    out=pt[:],
+                    lhsT=w_codes[h][:, c * P:(c + 1) * P].bitcast(E4M3),
+                    lhsT_scale=w_scales[h][:, c * P:(c + 1) * P],
+                    rhs=e_codes[g][:].bitcast(E5M2),
+                    rhs_scale=e_scales[g][:],
+                    start=True,
+                    stop=True,
+                )
+                pts[(n, c)] = pt
+
+        def sq(n, c):
+            hc = 4 * (n % 4) + c
+            tl = work.tile([P, D], F32, name="sq%d_%d" % (n, c), tag="sq", bufs=8)
+            nc.scalar.activation(out=tl[:], in_=pts[(n, c)][:], func=ACT.Square, bias=cst[:, hc:hc + 1], scale=1.0)
+            sqs[(n, c)] = tl
+
+        def kw(n, c):
+            hc = 4 * (n % 4) + c
+            tl = work.tile([P, D], F32, name="kw%d_%d" % (n, c), tag="kw", bufs=8)
+            if n >= KW_V_FROM and c >= 2:
+                nc.vector.tensor_scalar(
+                    out=tl[:], in0=pts[(n, c)][:], scalar1=w16[:, hc:hc + 1], scalar2=wbk[:, hc:hc + 1],
+                    op0=ALU.mult, op1=ALU.add,
+                )
+            else:
+                nc.scalar.activation(
+                    out=tl[:], in_=pts[(n, c)][:], func=ACT.Identity, bias=wbk[:, hc:hc + 1], scale=w16[:, hc:hc + 1]
+                )
+            kws[(n, c)] = tl
+
+        def acc_red_t(n):
+            acc = psum.tile([P, D], F32, name="acc%d" % n, tag="acc", bufs=1)
+            for t in range(4):
+                for c in range(4):
+                    nc.tensor.matmul(
+                        out=acc[:, t * P:(t + 1) * P], lhsT=sqs[(n, c)][:, t * P:(t + 1) * P], rhs=ident_f[:],
+                        is_transpose=True, start=(c == 0), stop=(c == 3),
+                    )
+            return acc
+
+        def red(n, acc):
+            nc.vector.tensor_reduce(
+                out=st8s[n][:, 0:4], in_=acc[:].rearrange("p (t m) -> p t m", t=4), axis=AX.X, op=ALU.add
+            )
+
+        def kb_stt(n, t):
+            g, h = divmod(n, 4)
+            kb = psum.tile([P, D], F32, name="kb%d_%d" % (n, t), tag="kb", bufs=3)
+            for c in range(4):
+                nc.tensor.transpose(kb[:, c * P:(c + 1) * P], kws[(n, c)][:, t * P:(t + 1) * P], ident_f[:])
+            junk = work.tile([P, D], F32, name="jv%d_%d" % (n, t), tag="junkv", bufs=2)
+            nc.vector.scalar_tensor_tensor(
+                out=junk[:], in0=kb[:], scalar=1.0, in1=hs[g][t][:, h * D:(h + 1) * D],
+                op0=ALU.mult, op1=ALU.mult, accum_out=tiny[("dot", n)][:, t:t + 1],
+            )
+
+        def value(g):
+            for t in range(4):
+                vp = psum.tile([P, D], F32, name="vp%d_%d" % (g, t), tag="kb", bufs=3)
+                nc.tensor.matmul_mx(
+                    out=vp[:],
+                    lhsT=e_codes[g][:, t * P:(t + 1) * P].bitcast(E5M2),
+                    lhsT_scale=e_scales[g][:, t * P:(t + 1) * P],
+                    rhs=w_codes[4][:].bitcast(E4M3),
+                    rhs_scale=w_scales[4][:],
+                    start=True,
+                    stop=True,
+                )
+                nc.vector.tensor_tensor(out=vals[g][:, t, :], in0=vp[:], in1=bvb[:], op=ALU.add)
+
+        def recip(n):
+            x8 = small("x8", n, 8)
+            nc.gpsimd.tensor_scalar(out=x8[:], in0=st8s[n][:], scalar1=C1, scalar2=C2, op0=ALU.mult, op1=ALU.add)
+            r8 = small("r8", n, 8)
+            nc.gpsimd.tensor_tensor(out=r8[:], in0=x8[:], in1=mone[:], op=ALU.pow)
+
+        def chain1(n, eng):
+            dot, r8 = tiny[("dot", n)], tiny[("r8", n)]
+            t1, t2, z4, r4 = small("t1", n, 4), small("t2", n, 4), small("z4", n, 4), small("r4", n, 4)
+            eng.tensor_tensor(out=t1[:], in0=dot[:], in1=r8[:, 0:4], op=ALU.mult)
+            eng.tensor_tensor(out=t2[:], in0=dot[:], in1=r8[:, 4:8], op=ALU.mult)
+            eng.tensor_tensor(out=z4[:], in0=t1[:], in1=t2[:], op=ALU.mult)
+            nc.gpsimd.tensor_tensor(out=r4[:], in0=z4[:], in1=quarter[:], op=ALU.pow)
+            m4 = small("m4", n, 4)
+            eng.tensor_scalar(out=m4[:], in0=r4[:], scalar1=CMIN, scalar2=None, op0=ALU.max)
+
+        def sign(n):
+            nc.scalar.activation(out=small("sg", n, 4)[:], in_=tiny[("dot", n)][:], func=ACT.Sign)
+
+        def chain2(n, eng):
+            eng.tensor_tensor(out=small("c4", n, 4)[:], in0=tiny[("m4", n)][:], in1=tiny[("sg", n)][:], op=ALU.mult)
+
+        def sigmoid(n):
+            nc.scalar.activation(out=small("gate", n, 4)[:], in_=tiny[("c4", n)][:], func=ACT.Sigmoid)
+
+        ots = {}
+
+        def out1(n, t, on_scalar, store):
+            g, h = divmod(n, 4)
+            if t == 0:
+                ots[n] = work.tile([P, 4, D], F32, name="ot%d" % n, tag="ot", bufs=3)
+            ot, gate = ots[n], tiny[("gate", n)]
+            if on_scalar:
+                nc.scalar.activation(out=ot[:, t, :], in_=vals[g][:, t, :], func=ACT.Copy, scale=gate[:, t:t + 1])
+            else:
+                nc.vector.tensor_scalar(
+                    out=ot[:, t, :], in0=vals[g][:, t, :], scalar1=gate[:, t:t + 1], scalar2=None, op0=ALU.mult
+                )
+            if store == 1:
+                nc.sync.dma_start(out=ov[g][:, t:t + 1, h, :], in_=ot[:, t:t + 1, :])
+            if store == 4:
+                nc.sync.dma_start(out=ov[g][:, :, h, :], in_=ot[:])
+
+        def outs(n):
+            for t in range(4):
+                out1(n, t, False, 4 if t == 3 else 0)
+
+        def recip_v(n):
+            x8 = small("x8", n, 8)
+            nc.vector.tensor_scalar(out=x8[:], in0=st8s[n][:], scalar1=C1, scalar2=C2, op0=ALU.mult, op1=ALU.add)
+            nc.vector.reciprocal(out=small("r8", n, 8)[:], in_=x8[:])
+
+        def fine_root(n, t):
+            dot, r8, y4, zc, r4 = [tiny[(nm, n)] for nm in ("dot", "r8", "y4", "zc", "r4")]
+            col = slice(t, t + 1)
+            nc.vector.tensor_scalar(
+                out=y4[:, col], in0=dot[:, col], scalar1=r8[:, col], scalar2=r8[:, 4 + t:5 + t], op0=ALU.mult, op1=ALU.mult
+            )
+            nc.vector.tensor_scalar(
+                out=zc[:, col], in0=y4[:, col], scalar1=dot[:, col], scalar2=1e-12, op0=ALU.mult, op1=ALU.max
+            )
+            nc.gpsimd.tensor_tensor(out=r4[:, col], in0=zc[:, col], in1=quarter[:, 0:1], op=ALU.pow)
+
+        def fine_sign(n, t):
+            nc.scalar.activation(out=tiny[("sg", n)][:, t:t + 1], in_=tiny[("dot", n)][:, t:t + 1], func=ACT.Sign)
+
+        def fine_gate(n, t):
+            nc.scalar.activation(
+                out=tiny[("gate", n)][:, t:t + 1], in_=tiny[("r4", n)][:, t:t + 1], func=ACT.Sigmoid,
+                scale=tiny[("sg", n)][:, t:t + 1],
+            )
+
+        fill = [(n, 0) for n in range(4)] + [(n, t) for n in range(4) for t in range(1, 4)]
+        fill += [(n, t) for n in range(4, 8) for t in range(4)]
+
+        done = [0]
+
+        def filler(k):
+            for n_t in fill[done[0]:done[0] + k]:
+                ssq(*n_t)
+            done[0] += k
+
+        filler(4)
+        prep("e", 0, False)
+        cst, w16, wbk = consts()
+        prep("w", 0, True)
+        mx(0)
+        prep("w", 1, False)
+        prep("w", 2, False)
+        for n in range(8):
+            small("dot", n, 4)
+            if n > 0:
+                chain1(n - 1, nc.gpsimd)
+            if n == 1:
+                prep("w", 4, False)
+                prep("w", 3, False)
+            if n == 2:
+                value(0)
+                prep("e", 1, False)
+            if n == 4:
+                value(1)
+            if n > 1:
+                outs(n - 2)
+            for c in range(4):
+                sq(n, c)
+            acc = acc_red_t(n)
+            for c in range(4):
+                kw(n, c)
+            if n < 7:
+                mx(n + 1)
+            red(n, acc)
+            if n == 7:
+                recip_v(n)
+            if n > 0:
+                sign(n - 1)
+                chain2(n - 1, nc.gpsimd)
+            filler(4)
+            if n < 7:
+                recip(n)
+            if n > 0:
+                sigmoid(n - 1)
+            if n == 7:
+                for nm in ("y4", "zc", "r4", "sg", "gate"):
+                    small(nm, n, 4)
+            for t in range(4):
+                kb_stt(n, t)
+                if n == 7:
+                    fine_root(n, t)
+        for what, t in (("o", 0), ("o", 1), ("s", 0), ("o", 2), ("g", 0), ("s", 1), ("o", 3), ("g", 1), ("s", 2), ("g", 2),
+                        ("s", 3), ("g", 3)):
+            if what == "o":
+                out1(6, t, True, 1)
+            elif what == "s":
+                fine_sign(7, t)
+            else:
+                fine_gate(7, t)
+        for t in range(4):
+            out1(7, t, False, 1)

@@ -81,7 +81,10 @@ def tile_engramgating_kernel(tc, embeddings, hidden_states, Wv, bv, Wk, bk, g1, 
                 nc.sync.dma_start(out=tl[:], in_=view[:, 2 * a:2 * a + 2, :])
                 raws[(kind, i, a)] = tl
 
-        load_hs(0, 0)
+        hs[0][0] = keep.tile([P, H * D], BF16, name="hs0_0")
+        for half in range(2):
+            cols = slice(1024 * half, 1024 * (half + 1))
+            nc.sync.dma_start(out=hs[0][0][:, cols], in_=hv[0, 0][:, cols])
         load_rows("e", 0)
         load_rows("w", 0)
         load_rows("w", 1)
@@ -236,14 +239,15 @@ def tile_engramgating_kernel(tc, embeddings, hidden_states, Wv, bv, Wk, bk, g1, 
             eng.tensor_tensor(out=t2[:], in0=dot[:], in1=r8[:, 4:8], op=ALU.mult)
             eng.tensor_tensor(out=z4[:], in0=t1[:], in1=t2[:], op=ALU.mult)
             nc.gpsimd.tensor_tensor(out=r4[:], in0=z4[:], in1=quarter[:], op=ALU.pow)
-            m4 = small("m4", n, 4)
-            eng.tensor_scalar(out=m4[:], in0=r4[:], scalar1=CMIN, scalar2=None, op0=ALU.max)
 
         def sign(n):
             nc.scalar.activation(out=small("sg", n, 4)[:], in_=tiny[("dot", n)][:], func=ACT.Sign)
 
-        def chain2(n, eng):
-            eng.tensor_tensor(out=small("c4", n, 4)[:], in0=tiny[("m4", n)][:], in1=tiny[("sg", n)][:], op=ALU.mult)
+        def chain2(n):
+            nc.vector.scalar_tensor_tensor(
+                out=small("c4", n, 4)[:], in0=tiny[("r4", n)][:], scalar=CMIN, in1=tiny[("sg", n)][:],
+                op0=ALU.max, op1=ALU.mult,
+            )
 
         def sigmoid(n):
             nc.scalar.activation(out=small("gate", n, 4)[:], in_=tiny[("c4", n)][:], func=ACT.Sigmoid)
@@ -314,8 +318,9 @@ def tile_engramgating_kernel(tc, embeddings, hidden_states, Wv, bv, Wk, bk, g1, 
         prep("w", 2, False)
         for n in range(8):
             small("dot", n, 4)
-            if n > 0:
-                chain1(n - 1, nc.gpsimd)
+            on_v = (2, 3) if n >= KW_V_FROM else ()
+            for c in on_v:
+                kw(n, c)
             if n == 1:
                 prep("w", 4, False)
                 prep("w", 3, False)
@@ -324,24 +329,24 @@ def tile_engramgating_kernel(tc, embeddings, hidden_states, Wv, bv, Wk, bk, g1, 
                 prep("e", 1, False)
             if n == 4:
                 value(1)
-            if n > 1:
-                outs(n - 2)
             for c in range(4):
                 sq(n, c)
+                if c == 1 and n > 0:
+                    sign(n - 1)
             acc = acc_red_t(n)
             for c in range(4):
-                kw(n, c)
+                if c not in on_v:
+                    kw(n, c)
             if n < 7:
                 mx(n + 1)
+            if n > 0:
+                chain2(n - 1)
+            if n > 1:
+                outs(n - 2)
             red(n, acc)
+            filler(4)
             if n == 7:
                 recip_v(n)
-            if n > 0:
-                sign(n - 1)
-                chain2(n - 1, nc.gpsimd)
-            filler(4)
-            if n < 7:
-                recip(n)
             if n > 0:
                 sigmoid(n - 1)
             if n == 7:
@@ -351,6 +356,9 @@ def tile_engramgating_kernel(tc, embeddings, hidden_states, Wv, bv, Wk, bk, g1, 
                 kb_stt(n, t)
                 if n == 7:
                     fine_root(n, t)
+            if n < 7:
+                recip_v(n)
+                chain1(n, nc.vector)
         for what, t in (("o", 0), ("o", 1), ("s", 0), ("o", 2), ("g", 0), ("s", 1), ("o", 3), ("g", 1), ("s", 2), ("g", 2),
                         ("s", 3), ("g", 3)):
             if what == "o":

@@ -56,6 +56,11 @@ def tile_engramgating_kernel(tc, embeddings, hidden_states, Wv, bv, Wk, bk, g1, 
         nc.gpsimd.memset(quarter[:], 0.25)
         mone = keep.tile([P, 8], F32, name="mone")
         nc.gpsimd.memset(mone[:], -1.0)
+        gwarm = keep.tile([P, 4], F32, name="gwarm")
+        nc.gpsimd.tensor_tensor(out=gwarm[:], in0=quarter[:], in1=quarter[:], op=ALU.pow)
+        nc.gpsimd.tensor_tensor(out=gwarm[:], in0=gwarm[:], in1=quarter[:], op=ALU.mult)
+        nc.gpsimd.tensor_scalar(out=gwarm[:], in0=gwarm[:], scalar1=C1, scalar2=C2, op0=ALU.mult, op1=ALU.add)
+        nc.gpsimd.tensor_scalar(out=gwarm[:], in0=gwarm[:], scalar1=CMIN, scalar2=None, op0=ALU.max)
         bvb = keep.tile([P, D], BF16, name="bvb")
 
         e_codes = [keep.tile([P, D], U32, name="e_codes%d" % g, align_bytes=64) for g in range(2)]
@@ -239,15 +244,14 @@ def tile_engramgating_kernel(tc, embeddings, hidden_states, Wv, bv, Wk, bk, g1, 
             eng.tensor_tensor(out=t2[:], in0=dot[:], in1=r8[:, 4:8], op=ALU.mult)
             eng.tensor_tensor(out=z4[:], in0=t1[:], in1=t2[:], op=ALU.mult)
             nc.gpsimd.tensor_tensor(out=r4[:], in0=z4[:], in1=quarter[:], op=ALU.pow)
+            m4 = small("m4", n, 4)
+            eng.tensor_scalar(out=m4[:], in0=r4[:], scalar1=CMIN, scalar2=None, op0=ALU.max)
 
         def sign(n):
             nc.scalar.activation(out=small("sg", n, 4)[:], in_=tiny[("dot", n)][:], func=ACT.Sign)
 
-        def chain2(n):
-            nc.vector.scalar_tensor_tensor(
-                out=small("c4", n, 4)[:], in0=tiny[("r4", n)][:], scalar=CMIN, in1=tiny[("sg", n)][:],
-                op0=ALU.max, op1=ALU.mult,
-            )
+        def chain2(n, eng):
+            eng.tensor_tensor(out=small("c4", n, 4)[:], in0=tiny[("m4", n)][:], in1=tiny[("sg", n)][:], op=ALU.mult)
 
         def sigmoid(n):
             nc.scalar.activation(out=small("gate", n, 4)[:], in_=tiny[("c4", n)][:], func=ACT.Sigmoid)
@@ -318,9 +322,8 @@ def tile_engramgating_kernel(tc, embeddings, hidden_states, Wv, bv, Wk, bk, g1, 
         prep("w", 2, False)
         for n in range(8):
             small("dot", n, 4)
-            on_v = (2, 3) if n >= KW_V_FROM else ()
-            for c in on_v:
-                kw(n, c)
+            if n > 0:
+                chain1(n - 1, nc.gpsimd)
             if n == 1:
                 prep("w", 4, False)
                 prep("w", 3, False)
@@ -331,34 +334,31 @@ def tile_engramgating_kernel(tc, embeddings, hidden_states, Wv, bv, Wk, bk, g1, 
                 value(1)
             for c in range(4):
                 sq(n, c)
-                if c == 1 and n > 0:
-                    sign(n - 1)
+                if c == 1 and n > 1:
+                    sigmoid(n - 2)
+                    outs(n - 2)
             acc = acc_red_t(n)
             for c in range(4):
-                if c not in on_v:
-                    kw(n, c)
+                kw(n, c)
             if n < 7:
                 mx(n + 1)
-            if n > 0:
-                chain2(n - 1)
-            if n > 1:
-                outs(n - 2)
             red(n, acc)
-            filler(4)
             if n == 7:
                 recip_v(n)
             if n > 0:
-                sigmoid(n - 1)
+                sign(n - 1)
+                chain2(n - 1, nc.gpsimd)
+            filler(4)
+            if n < 7:
+                recip(n)
             if n == 7:
+                sigmoid(n - 1)
                 for nm in ("y4", "zc", "r4", "sg", "gate"):
                     small(nm, n, 4)
             for t in range(4):
                 kb_stt(n, t)
                 if n == 7:
                     fine_root(n, t)
-            if n < 7:
-                recip_v(n)
-                chain1(n, nc.vector)
         for what, t in (("o", 0), ("o", 1), ("s", 0), ("o", 2), ("g", 0), ("s", 1), ("o", 3), ("g", 1), ("s", 2), ("g", 2),
                         ("s", 3), ("g", 3)):
             if what == "o":

@@ -40,18 +40,18 @@ def tile_engramgating_kernel(tc, embeddings, hidden_states, Wv, bv, Wk, bk, g1, 
         hv = hidden_states.rearrange("b s h d -> (b s) (h d)").rearrange("(g p t) c -> g t p c", g=2, p=P, t=4)
         ov = out.rearrange("b s h d -> (b s) h d").rearrange("(g p t) h d -> g p t h d", g=2, p=P, t=4)
 
-        craw = keep.tile([P, P], BF16, name="craw")
-        nc.gpsimd.memset(craw[:], 0.0)
-        for v, vec in enumerate((bk, g1, g2)):
-            nc.scalar.dma_start(out=craw[16 * v:16 * (v + 1), :], in_=vec.rearrange("h (c p) -> (h c) p", p=P))
-        warm = keep.tile([P, 1], F32, name="warm")
-        nc.gpsimd.memset(warm[:], 0.0)
-        warm2 = keep.tile([P, 1], F32, name="warm2")
-        nc.scalar.activation(out=warm2[:], in_=warm[:], func=ACT.Sigmoid)
         ident_f = keep.tile([P, P], F32, name="ident_f")
         make_identity(nc, ident_f[:])
         ident_b = keep.tile([P, P], BF16, name="ident_b")
         make_identity(nc, ident_b[:])
+        craw = keep.tile([P, P], BF16, name="craw")
+        nc.vector.memset(craw[64:128, :], 0.0)
+        for v, vec in enumerate((bk, g1, g2, bk)):
+            nc.scalar.dma_start(out=craw[16 * v:16 * (v + 1), :], in_=vec.rearrange("h (c p) -> (h c) p", p=P))
+        warm = keep.tile([P, 1], F32, name="warm")
+        nc.vector.memset(warm[:], 0.0)
+        warm2 = keep.tile([P, 1], F32, name="warm2")
+        nc.scalar.activation(out=warm2[:], in_=warm[:], func=ACT.Sigmoid)
         quarter = keep.tile([P, 4], F32, name="quarter")
         nc.gpsimd.memset(quarter[:], 0.25)
         mone = keep.tile([P, 8], F32, name="mone")

@@ -25,7 +25,7 @@ C2 = EPS * math.sqrt(512.0)
 CMIN = math.sqrt(1e-6)
 
 
-KW_V_FROM = 4
+KW_ON_VECTOR = (4, 5)
 
 
 def tile_engramgating_kernel(tc, embeddings, hidden_states, Wv, bv, Wk, bk, g1, g2, out):
@@ -40,18 +40,18 @@ def tile_engramgating_kernel(tc, embeddings, hidden_states, Wv, bv, Wk, bk, g1, 
         hv = hidden_states.rearrange("b s h d -> (b s) (h d)").rearrange("(g p t) c -> g t p c", g=2, p=P, t=4)
         ov = out.rearrange("b s h d -> (b s) h d").rearrange("(g p t) h d -> g p t h d", g=2, p=P, t=4)
 
+        craw = keep.tile([P, P], BF16, name="craw")
+        nc.gpsimd.memset(craw[:], 0.0)
+        for v, vec in enumerate((bk, g1, g2)):
+            nc.scalar.dma_start(out=craw[16 * v:16 * (v + 1), :], in_=vec.rearrange("h (c p) -> (h c) p", p=P))
+        warm = keep.tile([P, 1], F32, name="warm")
+        nc.gpsimd.memset(warm[:], 0.0)
+        warm2 = keep.tile([P, 1], F32, name="warm2")
+        nc.scalar.activation(out=warm2[:], in_=warm[:], func=ACT.Sigmoid)
         ident_f = keep.tile([P, P], F32, name="ident_f")
         make_identity(nc, ident_f[:])
         ident_b = keep.tile([P, P], BF16, name="ident_b")
         make_identity(nc, ident_b[:])
-        craw = keep.tile([P, P], BF16, name="craw")
-        nc.vector.memset(craw[64:128, :], 0.0)
-        for v, vec in enumerate((bk, g1, g2, bk)):
-            nc.scalar.dma_start(out=craw[16 * v:16 * (v + 1), :], in_=vec.rearrange("h (c p) -> (h c) p", p=P))
-        warm = keep.tile([P, 1], F32, name="warm")
-        nc.vector.memset(warm[:], 0.0)
-        warm2 = keep.tile([P, 1], F32, name="warm2")
-        nc.scalar.activation(out=warm2[:], in_=warm[:], func=ACT.Sigmoid)
         quarter = keep.tile([P, 4], F32, name="quarter")
         nc.gpsimd.memset(quarter[:], 0.25)
         mone = keep.tile([P, 8], F32, name="mone")
@@ -180,7 +180,7 @@ def tile_engramgating_kernel(tc, embeddings, hidden_states, Wv, bv, Wk, bk, g1, 
         def kw(n, c):
             hc = 4 * (n % 4) + c
             tl = work.tile([P, D], F32, name="kw%d_%d" % (n, c), tag="kw", bufs=8)
-            if n >= KW_V_FROM and c >= 2:
+            if n in KW_ON_VECTOR and c >= 2:
                 nc.vector.tensor_scalar(
                     out=tl[:], in0=pts[(n, c)][:], scalar1=w16[:, hc:hc + 1], scalar2=wbk[:, hc:hc + 1],
                     op0=ALU.mult, op1=ALU.add,
@@ -345,10 +345,11 @@ def tile_engramgating_kernel(tc, embeddings, hidden_states, Wv, bv, Wk, bk, g1, 
             red(n, acc)
             if n == 7:
                 recip_v(n)
+            filler(2)
             if n > 0:
                 sign(n - 1)
                 chain2(n - 1, nc.gpsimd)
-            filler(4)
+            filler(2)
             if n < 7:
                 recip(n)
             if n == 7:

@@ -25,7 +25,9 @@ C2 = EPS * math.sqrt(512.0)
 CMIN = math.sqrt(1e-6)
 
 
-KW_ON_VECTOR = (4, 5)
+KW_ON_VECTOR = (0, 0, 0, 0, 2, 2, 0, 2)
+FINE_STORE = (5,)
+LAST_ON_S = (0, 1)
 
 
 def tile_engramgating_kernel(tc, embeddings, hidden_states, Wv, bv, Wk, bk, g1, g2, out):
@@ -98,11 +100,11 @@ def tile_engramgating_kernel(tc, embeddings, hidden_states, Wv, bv, Wk, bk, g1, 
         load_hs(0, 2)
         load_hs(0, 3)
         load_rows("w", 4)
-        nc.sync.dma_start(out=bvb[:], in_=bv.partition_broadcast(P))
         load_rows("w", 3)
         load_rows("e", 1)
         for t in range(4):
             load_hs(1, t)
+        nc.sync.dma_start(out=bvb[:], in_=bv.partition_broadcast(P))
 
         def prep(kind, i, copy_on_scalar):
             codes, scales, fmt = (e_codes[i], e_scales[i], E5M2) if kind == "e" else (w_codes[i], w_scales[i], E4M3)
@@ -180,7 +182,7 @@ def tile_engramgating_kernel(tc, embeddings, hidden_states, Wv, bv, Wk, bk, g1, 
         def kw(n, c):
             hc = 4 * (n % 4) + c
             tl = work.tile([P, D], F32, name="kw%d_%d" % (n, c), tag="kw", bufs=8)
-            if n in KW_ON_VECTOR and c >= 2:
+            if c >= 4 - KW_ON_VECTOR[n]:
                 nc.vector.tensor_scalar(
                     out=tl[:], in0=pts[(n, c)][:], scalar1=w16[:, hc:hc + 1], scalar2=wbk[:, hc:hc + 1],
                     op0=ALU.mult, op1=ALU.add,
@@ -260,7 +262,7 @@ def tile_engramgating_kernel(tc, embeddings, hidden_states, Wv, bv, Wk, bk, g1, 
 
         def out1(n, t, on_scalar, store):
             g, h = divmod(n, 4)
-            if t == 0:
+            if n not in ots:
                 ots[n] = work.tile([P, 4, D], F32, name="ot%d" % n, tag="ot", bufs=3)
             ot, gate = ots[n], tiny[("gate", n)]
             if on_scalar:
@@ -276,7 +278,7 @@ def tile_engramgating_kernel(tc, embeddings, hidden_states, Wv, bv, Wk, bk, g1, 
 
         def outs(n):
             for t in range(4):
-                out1(n, t, False, 4 if t == 3 else 0)
+                out1(n, t, False, 1 if n in FINE_STORE else (4 if t == 3 else 0))
 
         def recip_v(n):
             x8 = small("x8", n, 8)
@@ -368,5 +370,8 @@ def tile_engramgating_kernel(tc, embeddings, hidden_states, Wv, bv, Wk, bk, g1, 
                 fine_sign(7, t)
             else:
                 fine_gate(7, t)
+                if t in LAST_ON_S:
+                    out1(7, t, True, 1)
         for t in range(4):
-            out1(7, t, False, 1)
+            if t not in LAST_ON_S:
+                out1(7, t, False, 1)

@@ -338,13 +338,16 @@ def tile_engramgating_kernel(tc, embeddings, hidden_states, Wv, bv, Wk, bk, g1, 
                 sq(n, c)
                 if c == 1 and n > 1:
                     sigmoid(n - 2)
-                    outs(n - 2)
+                    if n == 7:
+                        outs(n - 2)
             acc = acc_red_t(n)
             for c in range(4):
                 kw(n, c)
             if n < 7:
                 mx(n + 1)
             red(n, acc)
+            if 1 < n < 7:
+                outs(n - 2)
             if n == 7:
                 recip_v(n)
             filler(2)

@@ -28,6 +28,8 @@ CMIN = math.sqrt(1e-6)
 KW_ON_VECTOR = (0, 0, 0, 0, 2, 2, 0, 2)
 FINE_STORE = (5,)
 LAST_ON_S = (0, 1)
+LATE_UNTIL = 0
+RECIP_ON_V = False
 
 
 def tile_engramgating_kernel(tc, embeddings, hidden_states, Wv, bv, Wk, bk, g1, g2, out):
@@ -235,16 +237,21 @@ def tile_engramgating_kernel(tc, embeddings, hidden_states, Wv, bv, Wk, bk, g1, 
 
         def recip(n):
             x8 = small("x8", n, 8)
-            nc.gpsimd.tensor_scalar(out=x8[:], in0=st8s[n][:], scalar1=C1, scalar2=C2, op0=ALU.mult, op1=ALU.add)
-            r8 = small("r8", n, 8)
-            nc.gpsimd.tensor_tensor(out=r8[:], in0=x8[:], in1=mone[:], op=ALU.pow)
+            u4 = small("u4", n, 4)
+            if RECIP_ON_V:
+                nc.vector.tensor_scalar(out=x8[:], in0=st8s[n][:], scalar1=C1, scalar2=C2, op0=ALU.mult, op1=ALU.add)
+                nc.vector.tensor_tensor(out=u4[:], in0=x8[:, 0:4], in1=x8[:, 4:8], op=ALU.mult)
+                nc.vector.reciprocal(out=small("r8", n, 4)[:], in_=u4[:])
+            else:
+                nc.gpsimd.tensor_scalar(out=x8[:], in0=st8s[n][:], scalar1=C1, scalar2=C2, op0=ALU.mult, op1=ALU.add)
+                nc.gpsimd.tensor_tensor(out=u4[:], in0=x8[:, 0:4], in1=x8[:, 4:8], op=ALU.mult)
+                nc.gpsimd.tensor_tensor(out=small("r8", n, 4)[:], in0=u4[:], in1=mone[:, 0:4], op=ALU.pow)
 
         def chain1(n, eng):
             dot, r8 = tiny[("dot", n)], tiny[("r8", n)]
-            t1, t2, z4, r4 = small("t1", n, 4), small("t2", n, 4), small("z4", n, 4), small("r4", n, 4)
-            eng.tensor_tensor(out=t1[:], in0=dot[:], in1=r8[:, 0:4], op=ALU.mult)
-            eng.tensor_tensor(out=t2[:], in0=dot[:], in1=r8[:, 4:8], op=ALU.mult)
-            eng.tensor_tensor(out=z4[:], in0=t1[:], in1=t2[:], op=ALU.mult)
+            t1, z4, r4 = small("t1", n, 4), small("z4", n, 4), small("r4", n, 4)
+            eng.tensor_tensor(out=t1[:], in0=dot[:], in1=r8[:], op=ALU.mult)
+            eng.tensor_tensor(out=z4[:], in0=t1[:], in1=dot[:], op=ALU.mult)
             nc.gpsimd.tensor_tensor(out=r4[:], in0=z4[:], in1=quarter[:], op=ALU.pow)
             m4 = small("m4", n, 4)
             eng.tensor_scalar(out=m4[:], in0=r4[:], scalar1=CMIN, scalar2=None, op0=ALU.max)
@@ -336,26 +343,29 @@ def tile_engramgating_kernel(tc, embeddings, hidden_states, Wv, bv, Wk, bk, g1, 
                 value(1)
             for c in range(4):
                 sq(n, c)
-                if c == 1 and n > 1:
+                if c == 1 and n == 7:
                     sigmoid(n - 2)
-                    if n == 7:
-                        outs(n - 2)
-            acc = acc_red_t(n)
+                    outs(n - 2)
+            if n >= LATE_UNTIL:
+                acc = acc_red_t(n)
             for c in range(4):
                 kw(n, c)
             if n < 7:
                 mx(n + 1)
-            red(n, acc)
+            if LATE_UNTIL <= n < 7:
+                red(n, acc)
             if 1 < n < 7:
+                sigmoid(n - 2)
                 outs(n - 2)
             if n == 7:
+                red(n, acc)
                 recip_v(n)
             filler(2)
             if n > 0:
                 sign(n - 1)
                 chain2(n - 1, nc.gpsimd)
             filler(2)
-            if n < 7:
+            if LATE_UNTIL <= n < 7:
                 recip(n)
             if n == 7:
                 sigmoid(n - 1)
@@ -365,6 +375,10 @@ def tile_engramgating_kernel(tc, embeddings, hidden_states, Wv, bv, Wk, bk, g1, 
                 kb_stt(n, t)
                 if n == 7:
                     fine_root(n, t)
+            if n < LATE_UNTIL:
+                acc = acc_red_t(n)
+                red(n, acc)
+                recip(n)
         for what, t in (("o", 0), ("o", 1), ("s", 0), ("o", 2), ("g", 0), ("s", 1), ("o", 3), ("g", 1), ("s", 2), ("g", 2),
                         ("s", 3), ("g", 3)):
             if what == "o":

@@ -113,7 +113,7 @@ def tile_engramgating_kernel(tc, embeddings, hidden_states, Wv, bv, Wk, bk, g1, 
             xts = []
             for a in range(2):
                 words = raws[(kind, i, a)][:].rearrange("p t k -> p (t k)").bitcast(F32)
-                xt = psum.tile([P, D], F32, name="xt%s%d_%d" % (kind, i, a), tag="kb", bufs=3)
+                xt = psum.tile([P, D], F32, name="xt%s%d_%d" % (kind, i, a), tag="kb", bufs=4)
                 for tt in range(2):
                     for u in range(2):
                         j = 2 * tt + u
@@ -143,7 +143,7 @@ def tile_engramgating_kernel(tc, embeddings, hidden_states, Wv, bv, Wk, bk, g1, 
             return tl
 
         def consts():
-            cps = psum.tile([P, P], BF16, name="cps", tag="kb", bufs=3)
+            cps = psum.tile([P, P], BF16, name="cps", tag="kb", bufs=4)
             nc.tensor.transpose(cps[:], craw[:], ident_b[:])
             cst = keep.tile([P, 48], F32, name="cst")
             nc.vector.tensor_copy(out=cst[:], in_=cps[:, 0:48])
@@ -196,7 +196,7 @@ def tile_engramgating_kernel(tc, embeddings, hidden_states, Wv, bv, Wk, bk, g1, 
             kws[(n, c)] = tl
 
         def acc_red_t(n):
-            acc = psum.tile([P, D], F32, name="acc%d" % n, tag="acc", bufs=1)
+            acc = psum.tile([P, D], F32, name="acc%d" % n, tag="kb", bufs=4)
             for t in range(4):
                 for c in range(4):
                     nc.tensor.matmul(
@@ -212,7 +212,7 @@ def tile_engramgating_kernel(tc, embeddings, hidden_states, Wv, bv, Wk, bk, g1, 
 
         def kb_stt(n, t):
             g, h = divmod(n, 4)
-            kb = psum.tile([P, D], F32, name="kb%d_%d" % (n, t), tag="kb", bufs=3)
+            kb = psum.tile([P, D], F32, name="kb%d_%d" % (n, t), tag="kb", bufs=4)
             for c in range(4):
                 nc.tensor.transpose(kb[:, c * P:(c + 1) * P], kws[(n, c)][:, t * P:(t + 1) * P], ident_f[:])
             junk = work.tile([P, D], F32, name="jv%d_%d" % (n, t), tag="junkv", bufs=2)
@@ -223,7 +223,7 @@ def tile_engramgating_kernel(tc, embeddings, hidden_states, Wv, bv, Wk, bk, g1, 
 
         def value(g):
             for t in range(4):
-                vp = psum.tile([P, D], F32, name="vp%d_%d" % (g, t), tag="kb", bufs=3)
+                vp = psum.tile([P, D], F32, name="vp%d_%d" % (g, t), tag="kb", bufs=4)
                 nc.tensor.matmul_mx(
                     out=vp[:],
                     lhsT=e_codes[g][:, t * P:(t + 1) * P].bitcast(E5M2),

@@ -30,6 +30,10 @@ FINE_STORE = (5,)
 LAST_ON_S = (0, 1)
 LATE_UNTIL = 0
 RECIP_ON_V = False
+W0S = True
+HEADFILL = (4, 2, 2)
+LOADS = (("h", 0, 0, 0), ("h", 0, 0, 1), ("e", 0), ("h", 0, 1, 0), ("w", 0), ("h", 0, 1, 1), ("w", 1), ("H", 0, 2), ("w", 2), ("H", 0, 3), ("w", 4), ("w", 3), ("e", 1), ("H", 1, 0), ("H", 1, 1), ("H", 1, 2), ("H", 1, 3))
+FILL_TABLE = ((1, 2), (1, 2), (1, 2), (1, 2), (1, 2), (1, 2), (1, 1), (2, 2))
 
 
 def tile_engramgating_kernel(tc, embeddings, hidden_states, Wv, bv, Wk, bk, g1, g2, out):
@@ -90,22 +94,19 @@ def tile_engramgating_kernel(tc, embeddings, hidden_states, Wv, bv, Wk, bk, g1, 
                 nc.sync.dma_start(out=tl[:], in_=view[:, 2 * a:2 * a + 2, :])
                 raws[(kind, i, a)] = tl
 
-        hs[0][0] = keep.tile([P, H * D], BF16, name="hs0_0")
-        for half in range(2):
+        def load_half(g, t, half):
+            if hs[g][t] is None:
+                hs[g][t] = keep.tile([P, H * D], BF16, name="hs%d_%d" % (g, t))
             cols = slice(1024 * half, 1024 * (half + 1))
-            nc.sync.dma_start(out=hs[0][0][:, cols], in_=hv[0, 0][:, cols])
-        load_rows("e", 0)
-        load_rows("w", 0)
-        load_rows("w", 1)
-        load_hs(0, 1)
-        load_rows("w", 2)
-        load_hs(0, 2)
-        load_hs(0, 3)
-        load_rows("w", 4)
-        load_rows("w", 3)
-        load_rows("e", 1)
-        for t in range(4):
-            load_hs(1, t)
+            nc.sync.dma_start(out=hs[g][t][:, cols], in_=hv[g, t][:, cols])
+
+        for item in LOADS:
+            if item[0] == "h":
+                load_half(item[1], item[2], item[3])
+            elif item[0] == "H":
+                load_hs(item[1], item[2])
+            else:
+                load_rows(item[0], item[1])
         nc.sync.dma_start(out=bvb[:], in_=bv.partition_broadcast(P))
 
         def prep(kind, i, copy_on_scalar):
@@ -287,10 +288,13 @@ def tile_engramgating_kernel(tc, embeddings, hidden_states, Wv, bv, Wk, bk, g1, 
             for t in range(4):
                 out1(n, t, False, 1 if n in FINE_STORE else (4 if t == 3 else 0))
 
-        def recip_v(n):
-            x8 = small("x8", n, 8)
-            nc.vector.tensor_scalar(out=x8[:], in0=st8s[n][:], scalar1=C1, scalar2=C2, op0=ALU.mult, op1=ALU.add)
-            nc.vector.reciprocal(out=small("r8", n, 8)[:], in_=x8[:])
+        def recip_v(n, half):
+            if half == 0:
+                small("x8", n, 8)
+                small("r8", n, 8)
+            cols = slice(4 * half, 4 * half + 4)
+            nc.vector.tensor_scalar(out=tiny[("x8", n)][:, cols], in0=st8s[n][:, cols], scalar1=C1, scalar2=C2, op0=ALU.mult, op1=ALU.add)
+            nc.vector.reciprocal(out=tiny[("r8", n)][:, cols], in_=tiny[("x8", n)][:, cols])
 
         def fine_root(n, t):
             dot, r8, y4, zc, r4 = [tiny[(nm, n)] for nm in ("dot", "r8", "y4", "zc", "r4")]
@@ -312,7 +316,7 @@ def tile_engramgating_kernel(tc, embeddings, hidden_states, Wv, bv, Wk, bk, g1, 
                 scale=tiny[("sg", n)][:, t:t + 1],
             )
 
-        fill = [(n, 0) for n in range(4)] + [(n, t) for n in range(4) for t in range(1, 4)]
+        fill = [(n, t) for t in range(2) for n in range(4)] + [(n, t) for n in range(4) for t in (2, 3)]
         fill += [(n, t) for n in range(4, 8) for t in range(4)]
 
         done = [0]
@@ -322,10 +326,14 @@ def tile_engramgating_kernel(tc, embeddings, hidden_states, Wv, bv, Wk, bk, g1, 
                 ssq(*n_t)
             done[0] += k
 
-        filler(4)
+        FILLS = FILL_TABLE
+
+        filler(HEADFILL[0])
         prep("e", 0, False)
         cst, w16, wbk = consts()
-        prep("w", 0, True)
+        filler(HEADFILL[1])
+        prep("w", 0, W0S)
+        filler(HEADFILL[2])
         mx(0)
         prep("w", 1, False)
         prep("w", 2, False)
@@ -359,12 +367,12 @@ def tile_engramgating_kernel(tc, embeddings, hidden_states, Wv, bv, Wk, bk, g1, 
                 outs(n - 2)
             if n == 7:
                 red(n, acc)
-                recip_v(n)
-            filler(2)
+                recip_v(n, 0)
+            filler(FILLS[n][0])
             if n > 0:
                 sign(n - 1)
                 chain2(n - 1, nc.gpsimd)
-            filler(2)
+            filler(FILLS[n][1])
             if LATE_UNTIL <= n < 7:
                 recip(n)
             if n == 7:
@@ -374,6 +382,8 @@ def tile_engramgating_kernel(tc, embeddings, hidden_states, Wv, bv, Wk, bk, g1, 
             for t in range(4):
                 kb_stt(n, t)
                 if n == 7:
+                    if t == 0:
+                        recip_v(n, 1)
                     fine_root(n, t)
             if n < LATE_UNTIL:
                 acc = acc_red_t(n)

@@ -31,9 +31,10 @@ LAST_ON_S = (0, 1)
 LATE_UNTIL = 0
 RECIP_ON_V = False
 W0S = True
+DUMMY_ACC = 2
 HEADFILL = (4, 2, 2)
 LOADS = (("h", 0, 0, 0), ("h", 0, 0, 1), ("e", 0), ("h", 0, 1, 0), ("w", 0), ("h", 0, 1, 1), ("w", 1), ("H", 0, 2), ("w", 2), ("H", 0, 3), ("w", 4), ("w", 3), ("e", 1), ("H", 1, 0), ("H", 1, 1), ("H", 1, 2), ("H", 1, 3))
-FILL_TABLE = ((1, 2), (1, 2), (1, 2), (1, 2), (1, 2), (1, 2), (1, 1), (2, 2))
+FILL_TABLE = ((3, 0), (3, 0), (3, 0), (3, 0), (3, 0), (3, 0), (2, 0), (2, 2))
 
 
 def tile_engramgating_kernel(tc, embeddings, hidden_states, Wv, bv, Wk, bk, g1, g2, out):
@@ -196,8 +197,27 @@ def tile_engramgating_kernel(tc, embeddings, hidden_states, Wv, bv, Wk, bk, g1, 
                 )
             kws[(n, c)] = tl
 
-        def acc_red_t(n):
+        def acc_alloc(n, d):
+            g, h = divmod(n, 4)
             acc = psum.tile([P, D], F32, name="acc%d" % n, tag="kb", bufs=4)
+            for rep in range(d):
+                nc.tensor.matmul_mx(
+                    out=acc[:],
+                    lhsT=w_codes[h][:, 0:P].bitcast(E4M3),
+                    lhsT_scale=w_scales[h][:, 0:P],
+                    rhs=e_codes[g][:].bitcast(E5M2),
+                    rhs_scale=e_scales[g][:],
+                    start=True,
+                    stop=True,
+                )
+            accs[n] = acc
+
+        accs = {}
+
+        def acc_red_t(n):
+            if n not in accs:
+                acc_alloc(n, 0)
+            acc = accs[n]
             for t in range(4):
                 for c in range(4):
                     nc.tensor.matmul(
@@ -349,6 +369,8 @@ def tile_engramgating_kernel(tc, embeddings, hidden_states, Wv, bv, Wk, bk, g1, 
                 prep("e", 1, False)
             if n == 4:
                 value(1)
+            if n >= 1 and DUMMY_ACC:
+                acc_alloc(n, DUMMY_ACC)
             for c in range(4):
                 sq(n, c)
                 if c == 1 and n == 7:

@@ -162,9 +162,9 @@ def tile_engramgating_kernel(tc, embeddings, hidden_states, Wv, bv, Wk, bk, g1, 
                 out=junk[:], in_=hs[g][t][:, h * D:(h + 1) * D], func=ACT.Square, accum_out=st8s[n][:, 4 + t:5 + t]
             )
 
-        def mx(n):
+        def mx(n, cs=(0, 1, 2, 3)):
             g, h = divmod(n, 4)
-            for c in range(4):
+            for c in cs:
                 pt = psum.tile([P, D], F32, name="pt%d_%d" % (n, c), tag="pt", bufs=4)
                 nc.tensor.matmul_mx(
                     out=pt[:],
@@ -381,7 +381,7 @@ def tile_engramgating_kernel(tc, embeddings, hidden_states, Wv, bv, Wk, bk, g1, 
             for c in range(4):
                 kw(n, c)
             if n < 7:
-                mx(n + 1)
+                mx(n + 1, (0, 1, 2))
             if LATE_UNTIL <= n < 7:
                 red(n, acc)
             if 1 < n < 7:
@@ -402,6 +402,8 @@ def tile_engramgating_kernel(tc, embeddings, hidden_states, Wv, bv, Wk, bk, g1, 
                 for nm in ("y4", "zc", "r4", "sg", "gate"):
                     small(nm, n, 4)
             for t in range(4):
+                if n < 7 and t == 3:
+                    mx(n + 1, (3,))
                 kb_stt(n, t)
                 if n == 7:
                     if t == 0:

from contextlib import ExitStack
import math

import concourse.mybir as mybir
from concourse.masks import make_identity

FLOPS = 2 * 1024 * 512 * 2560

F32 = mybir.dt.float32
BF16 = mybir.dt.bfloat16
U32 = mybir.dt.uint32
U8 = mybir.dt.uint8
E5M2 = mybir.dt.float8_e5m2_x4
E4M3 = mybir.dt.float8_e4m3fn_x4
ACT = mybir.ActivationFunctionType
ALU = mybir.AluOpType
AX = mybir.AxisListType

P = 128
D = 512
H = 4
EPS = 2.0 ** -23
C1 = 1.0 / math.sqrt(512.0)
C2 = EPS * math.sqrt(512.0)
CMIN = math.sqrt(1e-6)


KW_ON_VECTOR = (0, 0, 0, 0, 2, 2, 0, 2)
FINE_STORE = (5,)
LAST_ON_S = (0, 1)
LATE_UNTIL = 0
RECIP_ON_V = False
W0S = True
DUMMY_ACC = 2
HEADFILL = (4, 2, 2)
LOADS = (("h", 0, 0, 0), ("h", 0, 0, 1), ("e", 0), ("h", 0, 1, 0), ("w", 0), ("h", 0, 1, 1), ("w", 1), ("H", 0, 2), ("w", 2), ("H", 0, 3), ("w", 4), ("w", 3), ("e", 1), ("H", 1, 0), ("H", 1, 1), ("H", 1, 2), ("H", 1, 3))
FILL_TABLE = ((3, 0), (3, 0), (3, 0), (3, 0), (3, 0), (3, 0), (2, 0), (2, 2))


def tile_engramgating_kernel(tc, embeddings, hidden_states, Wv, bv, Wk, bk, g1, g2, out):
    nc = tc.nc
    with ExitStack() as ctx:
        keep = ctx.enter_context(tc.tile_pool(name="keep", bufs=1))
        work = ctx.enter_context(tc.tile_pool(name="work", bufs=2))
        psum = ctx.enter_context(tc.psum_pool(name="psum", bufs=1))
        ctx.enter_context(tc.manual_schedule())

        ev = embeddings.rearrange("b s k -> (b s) k").rearrange("(g p t) k -> g p t k", g=2, p=P, t=4)
        hv = hidden_states.rearrange("b s h d -> (b s) (h d)").rearrange("(g p t) c -> g t p c", g=2, p=P, t=4)
        ov = out.rearrange("b s h d -> (b s) h d").rearrange("(g p t) h d -> g p t h d", g=2, p=P, t=4)

        craw = keep.tile([P, P], BF16, name="craw")
        nc.gpsimd.memset(craw[:], 0.0)
        for v, vec in enumerate((bk, g1, g2)):
            nc.scalar.dma_start(out=craw[16 * v:16 * (v + 1), :], in_=vec.rearrange("h (c p) -> (h c) p", p=P))
        warm = keep.tile([P, 1], F32, name="warm")
        nc.gpsimd.memset(warm[:], 0.0)
        warm2 = keep.tile([P, 1], F32, name="warm2")
        nc.scalar.activation(out=warm2[:], in_=warm[:], func=ACT.Sigmoid)
        ident_f = keep.tile([P, P], F32, name="ident_f")
        make_identity(nc, ident_f[:])
        ident_b = keep.tile([P, P], BF16, name="ident_b")
        make_identity(nc, ident_b[:])
        quarter = keep.tile([P, 4], F32, name="quarter")
        nc.gpsimd.memset(quarter[:], 0.25)
        mone = keep.tile([P, 8], F32, name="mone")
        nc.gpsimd.memset(mone[:], -1.0)
        gwarm = keep.tile([P, 4], F32, name="gwarm")
        nc.gpsimd.tensor_tensor(out=gwarm[:], in0=quarter[:], in1=quarter[:], op=ALU.pow)
        nc.gpsimd.tensor_tensor(out=gwarm[:], in0=gwarm[:], in1=quarter[:], op=ALU.mult)
        nc.gpsimd.tensor_scalar(out=gwarm[:], in0=gwarm[:], scalar1=C1, scalar2=C2, op0=ALU.mult, op1=ALU.add)
        nc.gpsimd.tensor_scalar(out=gwarm[:], in0=gwarm[:], scalar1=CMIN, scalar2=None, op0=ALU.max)
        bvb = keep.tile([P, D], BF16, name="bvb")

        e_codes = [keep.tile([P, D], U32, name="e_codes%d" % g, align_bytes=64) for g in range(2)]
        e_scales = [keep.tile([P, D], U8, name="e_scales%d" % g, align_bytes=64) for g in range(2)]
        w_codes = [keep.tile([P, D], U32, name="w_codes%d" % i, align_bytes=64) for i in range(5)]
        w_scales = [keep.tile([P, D], U8, name="w_scales%d" % i, align_bytes=64) for i in range(5)]

        hs = [[None] * 4, [None] * 4]
        raws = {}

        def load_hs(g, t):
            tl = keep.tile([P, H * D], BF16, name="hs%d_%d" % (g, t))
            nc.sync.dma_start(out=tl[:], in_=hv[g, t])
            hs[g][t] = tl

        def load_rows(kind, i):
            if kind == "e":
                view = ev[i]
            else:
                view = (Wv if i == 4 else Wk[i]).rearrange("(c p) k -> p c k", p=P)
            for a in range(2):
                tl = work.tile([P, 2, D], BF16, name="raw%s%d_%d" % (kind, i, a), tag="raw", bufs=14)
                nc.sync.dma_start(out=tl[:], in_=view[:, 2 * a:2 * a + 2, :])
                raws[(kind, i, a)] = tl

        def load_half(g, t, half):
            if hs[g][t] is None:
                hs[g][t] = keep.tile([P, H * D], BF16, name="hs%d_%d" % (g, t))
            cols = slice(1024 * half, 1024 * (half + 1))
            nc.sync.dma_start(out=hs[g][t][:, cols], in_=hv[g, t][:, cols])

        for item in LOADS:
            if item[0] == "h":
                load_half(item[1], item[2], item[3])
            elif item[0] == "H":
                load_hs(item[1], item[2])
            else:
                load_rows(item[0], item[1])
        nc.sync.dma_start(out=bvb[:], in_=bv.partition_broadcast(P))

        def prep(kind, i, copy_on_scalar):
            codes, scales, fmt = (e_codes[i], e_scales[i], E5M2) if kind == "e" else (w_codes[i], w_scales[i], E4M3)
            xts = []
            for a in range(2):
                words = raws[(kind, i, a)][:].rearrange("p t k -> p (t k)").bitcast(F32)
                xt = psum.tile([P, D], F32, name="xt%s%d_%d" % (kind, i, a), tag="kb", bufs=4)
                for tt in range(2):
                    for u in range(2):
                        j = 2 * tt + u
                        nc.tensor.transpose(xt[:, j * P:(j + 1) * P], words[:, 256 * tt + u:256 * (tt + 1):2], ident_f[:])
                xts.append(xt)
            grps = []
            for a in range(2):
                grp = work.tile([P, 1024], BF16, name="grp%s%d_%d" % (kind, i, a), tag="grp", bufs=4, align_bytes=64)
                dst = grp[:].bitcast(F32).rearrange("p (tt r u) -> p tt r u", tt=2, u=2)
                srcv = xts[a][:].rearrange("p (tt u r) -> p tt r u", tt=2, u=2)
                if copy_on_scalar:
                    nc.scalar.copy(out=dst, in_=srcv)
                else:
                    nc.vector.tensor_copy(out=dst, in_=srcv)
                grps.append(grp)
            for a in range(2):
                cols = slice(256 * a, 256 * (a + 1))
                nc.vector.quantize_mx(out=codes[:, cols].bitcast(fmt), scales=scales[:, cols], in_=grps[a][:])

        st8s = [keep.tile([P, 8], F32, name="st8_%d" % n) for n in range(8)]
        vals = [keep.tile([P, 4, D], F32, name="val%d" % g) for g in range(2)]
        pts, sqs, kws, tiny = {}, {}, {}, {}

        def small(nm, n, w):
            tl = keep.tile([P, w], F32, name="%s_%d" % (nm, n))
            tiny[(nm, n)] = tl
            return tl

        def consts():
            cps = psum.tile([P, P], BF16, name="cps", tag="kb", bufs=4)
            nc.tensor.transpose(cps[:], craw[:], ident_b[:])
            cst = keep.tile([P, 48], F32, name="cst")
            nc.vector.tensor_copy(out=cst[:], in_=cps[:, 0:48])
            w16 = keep.tile([P, 16], F32, name="w16")
            nc.vector.tensor_tensor(out=w16[:], in0=cst[:, 16:32], in1=cst[:, 32:48], op=ALU.mult)
            wbk = keep.tile([P, 16], F32, name="wbk")
            nc.vector.tensor_tensor(out=wbk[:], in0=w16[:], in1=cst[:, 0:16], op=ALU.mult)
            return cst, w16, wbk

        def ssq(n, t):
            g, h = divmod(n, 4)
            junk = work.tile([P, D], F32, name="js%d_%d" % (n, t), tag="junks", bufs=2)
            nc.scalar.activation(
                out=junk[:], in_=hs[g][t][:, h * D:(h + 1) * D], func=ACT.Square, accum_out=st8s[n][:, 4 + t:5 + t]
            )

        def mx(n, cs=(0, 1, 2, 3)):
            g, h = divmod(n, 4)
            for c in cs:
                pt = psum.tile([P, D], F32, name="pt%d_%d" % (n, c), tag="pt", bufs=4)
                nc.tensor.matmul_mx(
                    out=pt[:],
                    lhsT=w_codes[h][:, c * P:(c + 1) * P].bitcast(E4M3),
                    lhsT_scale=w_scales[h][:, c * P:(c + 1) * P],
                    rhs=e_codes[g][:].bitcast(E5M2),
                    rhs_scale=e_scales[g][:],
                    start=True,
                    stop=True,
                )
                pts[(n, c)] = pt

        def sq(n, c):
            hc = 4 * (n % 4) + c
            tl = work.tile([P, D], F32, name="sq%d_%d" % (n, c), tag="sq", bufs=8)
            nc.scalar.activation(out=tl[:], in_=pts[(n, c)][:], func=ACT.Square, bias=cst[:, hc:hc + 1], scale=1.0)
            sqs[(n, c)] = tl

        def kw(n, c):
            hc = 4 * (n % 4) + c
            tl = work.tile([P, D], F32, name="kw%d_%d" % (n, c), tag="kw", bufs=8)
            if c >= 4 - KW_ON_VECTOR[n]:
                nc.vector.tensor_scalar(
                    out=tl[:], in0=pts[(n, c)][:], scalar1=w16[:, hc:hc + 1], scalar2=wbk[:, hc:hc + 1],
                    op0=ALU.mult, op1=ALU.add,
                )
            else:
                nc.scalar.activation(
                    out=tl[:], in_=pts[(n, c)][:], func=ACT.Identity, bias=wbk[:, hc:hc + 1], scale=w16[:, hc:hc + 1]
                )
            kws[(n, c)] = tl

        def acc_alloc(n, d):
            g, h = divmod(n, 4)
            acc = psum.tile([P, D], F32, name="acc%d" % n, tag="kb", bufs=4)
            for rep in range(d):
                nc.tensor.matmul_mx(
                    out=acc[:],
                    lhsT=w_codes[h][:, 0:P].bitcast(E4M3),
                    lhsT_scale=w_scales[h][:, 0:P],
                    rhs=e_codes[g][:].bitcast(E5M2),
                    rhs_scale=e_scales[g][:],
                    start=True,
                    stop=True,
                )
            accs[n] = acc

        accs = {}

        def acc_red_t(n):
            if n not in accs:
                acc_alloc(n, 0)
            acc = accs[n]
            for t in range(4):
                for c in range(4):
                    nc.tensor.matmul(
                        out=acc[:, t * P:(t + 1) * P], lhsT=sqs[(n, c)][:, t * P:(t + 1) * P], rhs=ident_f[:],
                        is_transpose=True, start=(c == 0), stop=(c == 3),
                    )
            return acc

        def red(n, acc):
            nc.vector.tensor_reduce(
                out=st8s[n][:, 0:4], in_=acc[:].rearrange("p (t m) -> p t m", t=4), axis=AX.X, op=ALU.add
            )

        def kb_stt(n, t):
            g, h = divmod(n, 4)
            kb = psum.tile([P, D], F32, name="kb%d_%d" % (n, t), tag="kb", bufs=4)
            for c in range(4):
                nc.tensor.transpose(kb[:, c * P:(c + 1) * P], kws[(n, c)][:, t * P:(t + 1) * P], ident_f[:])
            junk = work.tile([P, D], F32, name="jv%d_%d" % (n, t), tag="junkv", bufs=2)
            nc.vector.scalar_tensor_tensor(
                out=junk[:], in0=kb[:], scalar=1.0, in1=hs[g][t][:, h * D:(h + 1) * D],
                op0=ALU.mult, op1=ALU.mult, accum_out=tiny[("dot", n)][:, t:t + 1],
            )

        def value(g):
            for t in range(4):
                vp = psum.tile([P, D], F32, name="vp%d_%d" % (g, t), tag="kb", bufs=4)
                nc.tensor.matmul_mx(
                    out=vp[:],
                    lhsT=e_codes[g][:, t * P:(t + 1) * P].bitcast(E5M2),
                    lhsT_scale=e_scales[g][:, t * P:(t + 1) * P],
                    rhs=w_codes[4][:].bitcast(E4M3),
                    rhs_scale=w_scales[4][:],
                    start=True,
                    stop=True,
                )
                nc.vector.tensor_tensor(out=vals[g][:, t, :], in0=vp[:], in1=bvb[:], op=ALU.add)

        def recip(n):
            x8 = small("x8", n, 8)
            u4 = small("u4", n, 4)
            if RECIP_ON_V:
                nc.vector.tensor_scalar(out=x8[:], in0=st8s[n][:], scalar1=C1, scalar2=C2, op0=ALU.mult, op1=ALU.add)
                nc.vector.tensor_tensor(out=u4[:], in0=x8[:, 0:4], in1=x8[:, 4:8], op=ALU.mult)
                nc.vector.reciprocal(out=small("r8", n, 4)[:], in_=u4[:])
            else:
                nc.gpsimd.tensor_scalar(out=x8[:], in0=st8s[n][:], scalar1=C1, scalar2=C2, op0=ALU.mult, op1=ALU.add)
                nc.gpsimd.tensor_tensor(out=u4[:], in0=x8[:, 0:4], in1=x8[:, 4:8], op=ALU.mult)
                nc.gpsimd.tensor_tensor(out=small("r8", n, 4)[:], in0=u4[:], in1=mone[:, 0:4], op=ALU.pow)

        def chain1(n, eng):
            dot, r8 = tiny[("dot", n)], tiny[("r8", n)]
            t1, z4, r4 = small("t1", n, 4), small("z4", n, 4), small("r4", n, 4)
            eng.tensor_tensor(out=t1[:], in0=dot[:], in1=r8[:], op=ALU.mult)
            eng.tensor_tensor(out=z4[:], in0=t1[:], in1=dot[:], op=ALU.mult)
            nc.gpsimd.tensor_tensor(out=r4[:], in0=z4[:], in1=quarter[:], op=ALU.pow)
            m4 = small("m4", n, 4)
            eng.tensor_scalar(out=m4[:], in0=r4[:], scalar1=CMIN, scalar2=None, op0=ALU.max)

        def sign(n):
            nc.scalar.activation(out=small("sg", n, 4)[:], in_=tiny[("dot", n)][:], func=ACT.Sign)

        def chain2(n, eng):
            eng.tensor_tensor(out=small("c4", n, 4)[:], in0=tiny[("m4", n)][:], in1=tiny[("sg", n)][:], op=ALU.mult)

        def sigmoid(n):
            nc.scalar.activation(out=small("gate", n, 4)[:], in_=tiny[("c4", n)][:], func=ACT.Sigmoid)

        ots = {}

        def out1(n, t, on_scalar, store):
            g, h = divmod(n, 4)
            if n not in ots:
                ots[n] = work.tile([P, 4, D], F32, name="ot%d" % n, tag="ot", bufs=3)
            ot, gate = ots[n], tiny[("gate", n)]
            if on_scalar:
                nc.scalar.activation(out=ot[:, t, :], in_=vals[g][:, t, :], func=ACT.Copy, scale=gate[:, t:t + 1])
            else:
                nc.vector.tensor_scalar(
                    out=ot[:, t, :], in0=vals[g][:, t, :], scalar1=gate[:, t:t + 1], scalar2=None, op0=ALU.mult
                )
            if store == 1:
                nc.sync.dma_start(out=ov[g][:, t:t + 1, h, :], in_=ot[:, t:t + 1, :])
            if store == 4:
                nc.sync.dma_start(out=ov[g][:, :, h, :], in_=ot[:])

        def outs(n):
            for t in range(4):
                out1(n, t, False, 1 if n in FINE_STORE else (4 if t == 3 else 0))

        def recip_v(n, half):
            if half == 0:
                small("x8", n, 8)
                small("r8", n, 8)
            cols = slice(4 * half, 4 * half + 4)
            nc.vector.tensor_scalar(out=tiny[("x8", n)][:, cols], in0=st8s[n][:, cols], scalar1=C1, scalar2=C2, op0=ALU.mult, op1=ALU.add)
            nc.vector.reciprocal(out=tiny[("r8", n)][:, cols], in_=tiny[("x8", n)][:, cols])

        def fine_root(n, t):
            dot, r8, y4, zc, r4 = [tiny[(nm, n)] for nm in ("dot", "r8", "y4", "zc", "r4")]
            col = slice(t, t + 1)
            nc.vector.tensor_scalar(
                out=y4[:, col], in0=dot[:, col], scalar1=r8[:, col], scalar2=r8[:, 4 + t:5 + t], op0=ALU.mult, op1=ALU.mult
            )
            nc.vector.tensor_scalar(
                out=zc[:, col], in0=y4[:, col], scalar1=dot[:, col], scalar2=1e-12, op0=ALU.mult, op1=ALU.max
            )
            nc.gpsimd.tensor_tensor(out=r4[:, col], in0=zc[:, col], in1=quarter[:, 0:1], op=ALU.pow)

        def fine_sign(n, t):
            nc.scalar.activation(out=tiny[("sg", n)][:, t:t + 1], in_=tiny[("dot", n)][:, t:t + 1], func=ACT.Sign)

        def fine_gate(n, t):
            nc.scalar.activation(
                out=tiny[("gate", n)][:, t:t + 1], in_=tiny[("r4", n)][:, t:t + 1], func=ACT.Sigmoid,
                scale=tiny[("sg", n)][:, t:t + 1],
            )

        fill = [(n, t) for t in range(2) for n in range(4)] + [(n, t) for n in range(4) for t in (2, 3)]
        fill += [(n, t) for n in range(4, 8) for t in range(4)]

        done = [0]

        def filler(k):
            for n_t in fill[done[0]:done[0] + k]:
                ssq(*n_t)
            done[0] += k

        FILLS = FILL_TABLE

        filler(HEADFILL[0])
        prep("e", 0, False)
        cst, w16, wbk = consts()
        filler(HEADFILL[1])
        prep("w", 0, W0S)
        filler(HEADFILL[2])
        mx(0)
        prep("w", 1, False)
        prep("w", 2, False)
        for n in range(8):
            small("dot", n, 4)
            if n > 0:
                chain1(n - 1, nc.gpsimd)
            if n == 1:
                prep("w", 4, False)
                prep("w", 3, False)
            if n == 2:
                value(0)
                prep("e", 1, False)
            if n == 4:
                value(1)
            if n >= 1 and DUMMY_ACC:
                acc_alloc(n, DUMMY_ACC)
            for c in range(4):
                sq(n, c)
                if c == 1 and n == 7:
                    sigmoid(n - 2)
                    outs(n - 2)
            if n >= LATE_UNTIL:
                acc = acc_red_t(n)
            for c in range(4):
                kw(n, c)
            if n < 7:
                mx(n + 1, (0, 1, 2))
            if LATE_UNTIL <= n < 7:
                red(n, acc)
            if 1 < n < 7:
                sigmoid(n - 2)
                outs(n - 2)
            if n == 7:
                red(n, acc)
                recip_v(n, 0)
            filler(FILLS[n][0])
            if n > 0:
                sign(n - 1)
                chain2(n - 1, nc.gpsimd)
            filler(FILLS[n][1])
            if LATE_UNTIL <= n < 7:
                recip(n)
            if n == 7:
                sigmoid(n - 1)
                for nm in ("y4", "zc", "r4", "sg", "gate"):
                    small(nm, n, 4)
            for t in range(4):
                if n < 7 and t == 3:
                    mx(n + 1, (3,))
                kb_stt(n, t)
                if n == 7:
                    if t == 0:
                        recip_v(n, 1)
                    fine_root(n, t)
            if n < LATE_UNTIL:
                acc = acc_red_t(n)
                red(n, acc)
                recip(n)
        for what, t in (("o", 0), ("o", 1), ("s", 0), ("o", 2), ("g", 0), ("s", 1), ("o", 3), ("g", 1), ("s", 2), ("g", 2),
                        ("s", 3), ("g", 3)):
            if what == "o":
                out1(6, t, True, 1)
            elif what == "s":
                fine_sign(7, t)
            else:
                fine_gate(7, t)
                if t in LAST_ON_S:
                    out1(7, t, True, 1)
        for t in range(4):
            if t not in LAST_ON_S:
                out1(7, t, False, 1)
